import numpy as np
import ml_dtypes


def mxq(x, axis, fmt="e4m3"):
    dtype, down = {"e4m3": (ml_dtypes.float8_e4m3fn, 7), "e5m2": (ml_dtypes.float8_e5m2, 14)}[fmt]
    v = np.moveaxis(np.asarray(x, np.float32).astype(ml_dtypes.bfloat16).astype(np.float64), axis, -1)
    blocks = v.reshape(v.shape[:-1] + (-1, 32))
    amax = np.abs(blocks).max(-1, keepdims=True)
    byte = np.maximum(np.where(amax > 0, np.frexp(amax)[1] - 1 + 127, 0) - down, 1)
    scale = np.exp2(byte - 127.0)
    codes = (blocks / scale).astype(np.float32).astype(dtype).astype(np.float64)
    return np.moveaxis((codes * scale).reshape(v.shape), -1, axis)


WIDE = False


def mx_kscale(k):
    if not WIDE:
        return np.ones(k)
    levels = np.array([10, -10, 5, -5, 0])
    if k % 512:
        return np.exp2(np.random.permutation(np.resize(levels, k // 32))).repeat(32)
    a = np.empty((k // 512, 16))
    for p in range(k // 512):
        a[p, :8] = np.random.permutation(np.resize(levels, 8))
        for g in range(8):
            far = levels[np.abs(levels - a[p, g]) >= 10]
            a[p, g + 8] = far[np.random.randint(len(far))]
    return np.exp2(a.ravel()).repeat(32)


BF16 = ml_dtypes.bfloat16


def bf(x):
    return np.asarray(x, np.float32).astype(BF16)


def f64(x):
    return np.asarray(x).astype(np.float64)


E2M1 = np.array([0.0, 0.5, 1.0, 1.5, 2.0, 3.0, 4.0, 6.0, -0.0, -0.5, -1.0, -1.5, -2.0, -3.0, -4.0, -6.0])


def pack_weight(w, fmt):
    k, n = w.shape
    w = f64(bf(w)).reshape(k // 32, 32, n)
    amax = np.abs(w).max(1)
    if fmt == "e4m3":
        byte = np.frexp(amax)[1] - 1 + 127 - 7
    else:
        mant, ex = np.frexp(amax / 6.0)
        byte = np.where(mant > 0.5, ex, ex - 1) + 127
    byte = np.clip(np.where(amax > 0, byte, 1), 1, 254)
    scaled = (w * np.exp2(127.0 - byte)[:, None, :]).reshape(k, n).astype(np.float32)
    by_word = np.ascontiguousarray(scaled.reshape(k // 512, 128, 4, n).transpose(0, 1, 3, 2))
    if fmt == "e4m3":
        words = by_word.astype(ml_dtypes.float8_e4m3fn).view(np.uint8)
    else:
        c = by_word.astype(ml_dtypes.float4_e2m1fn).view(np.uint8) & 0xF
        words = c[..., 0::2] | (c[..., 1::2] << 4)
    return np.ascontiguousarray(words), np.ascontiguousarray(byte.astype(np.uint8).reshape(k // 512, 16, n))


def unpack_weight(words, scales, fmt):
    g, p, n, _ = words.shape
    if fmt == "e4m3":
        vals = np.ascontiguousarray(words).view(ml_dtypes.float8_e4m3fn).astype(np.float64)
    else:
        nib = np.empty((g, p, n, 4), np.uint8)
        nib[..., 0::2] = words & 0xF
        nib[..., 1::2] = words >> 4
        vals = E2M1[nib]
    vals = vals * np.repeat(np.exp2(scales.astype(np.float64) - 127.0), 8, axis=1)[..., None]
    return vals.transpose(0, 1, 3, 2).reshape(g * 512, n)


N, F, H = 1536, 512, 512
SIG = 1.5


def draw_adj():
    r = np.random.uniform(0.5, 1.5, (N, 1))
    return 2.0 * r * np.exp(SIG * np.random.standard_normal((N, N)) - 0.5 * SIG * SIG) / N


def setup_inputs():
    s, t = mx_kscale(F), mx_kscale(N)
    x_init = bf(np.random.standard_normal((N, F)) * s / t[:, None])
    adj1 = bf(draw_adj() * t)
    W1_words, W1_scales = pack_weight(np.random.standard_normal((F, H)) * 4.0 / np.sqrt(F) / s[:, None], "e4m3")
    b1 = bf(np.random.standard_normal(H) * 0.3)
    return {"x_init": x_init,
            "adj1": adj1,
            "W1_words": W1_words,
            "W1_scales": W1_scales,
            "b1": b1}


def reference(x_init, adj1, W1_words, W1_scales, b1):
    support = mxq(f64(x_init), 1, "e4m3") @ unpack_weight(W1_words, W1_scales, "e4m3")
    y = (mxq(f64(adj1), 1, "e4m3") @ mxq(support, 0, "e4m3")) + f64(b1)
    return np.maximum(y, 0.0)

@@ -1,0 +1,199 @@
+from contextlib import ExitStack
+
+import concourse.mybir as mybir
+from concourse.masks import make_identity
+
+F32 = mybir.dt.float32
+BF16 = mybir.dt.bfloat16
+I32 = mybir.dt.int32
+U32 = mybir.dt.uint32
+U8 = mybir.dt.uint8
+FP8X4 = mybir.dt.float8_e4m3fn_x4
+ALU = mybir.AluOpType
+ACT = mybir.ActivationFunctionType
+
+P = 128
+PACK = 4
+K_PASS = P * PACK
+NODES = 1536
+FEATURES = 512
+HIDDEN = 512
+NODE_PASSES = NODES // K_PASS
+ROW_TILES = NODES // P
+ROUND_TILES = 2
+ROUNDS = ROW_TILES // ROUND_TILES
+AHEAD = 3
+
+F32_MAX = 3.4028234663852886e38
+
+FLOPS = 2 * NODES * FEATURES * HIDDEN + 2 * NODES * NODES * HIDDEN
+
+
+def tile_gcn_pa_kernel(tc, x_init, adj1, W1_words, W1_scales, b1, out):
+    nc = tc.nc
+    with ExitStack() as ctx:
+        keep = ctx.enter_context(tc.tile_pool(name="keep", bufs=1))
+        banks = ctx.enter_context(tc.psum_pool(name="banks", bufs=8))
+        ctx.enter_context(tc.manual_schedule())
+
+        def empty_bank(index, dst, src):
+            if index % 2 == 0:
+                nc.scalar.copy(out=dst, in_=src)
+            else:
+                nc.vector.tensor_copy(out=dst, in_=src)
+
+        def quantise(grouped, codes, scales):
+            nc.vector.quantize_mx(
+                out=codes[:].bitcast(FP8X4),
+                scales=scales[:],
+                in_=grouped[:].rearrange("p c t -> p (c t)"),
+            )
+
+        ident = keep.tile([P, P], F32)
+        make_identity(nc, ident[:])
+        ones = keep.tile([P, P], BF16)
+        nc.vector.memset(ones[:], 1.0)
+        bias_row = keep.tile([P, HIDDEN], BF16)
+        nc.vector.memset(bias_row[:], 0.0)
+        nc.scalar.dma_start(out=bias_row[0:1, :], in_=b1.rearrange("(o h) -> o h", o=1))
+        warm = keep.tile([P, 1], F32)
+        nc.vector.memset(warm[:], 0.0)
+        nc.scalar.activation(out=warm[:], in_=warm[:], func=ACT.Relu)
+
+        w_scales = keep.tile([P, HIDDEN], U8, align_bytes=64)
+        nc.vector.memset(w_scales[:].bitcast(I32), 0)
+
+        x_chunks = x_init.rearrange("(g p u e) f -> g u p e f", p=P, u=2, e=2)
+        x_sb = []
+        for a in range(2 * NODE_PASSES):
+            chunk = keep.tile([P, 2, FEATURES], BF16, name="x_sb%d" % a)
+            nc.sync.dma_start(out=chunk[:], in_=x_chunks[a // 2, a % 2])
+            x_sb.append(chunk)
+        for quadrant in range(4):
+            nc.sync.dma_start(
+                out=w_scales[32 * quadrant : 32 * quadrant + 4, :].bitcast(I32),
+                in_=W1_scales[0, 4 * quadrant : 4 * quadrant + 4, :].bitcast(I32),
+            )
+        w_codes = keep.tile([P, HIDDEN], U32, align_bytes=64)
+        nc.sync.dma_start(out=w_codes[:].bitcast(I32), in_=W1_words[0].rearrange("p n t -> p (n t)").bitcast(I32))
+        adj_rows = adj1.rearrange("(p r) k -> p r k", r=ROW_TILES)
+        out_rows = out.rearrange("(p r) h -> p r h", r=ROW_TILES)
+        adj_sb = []
+        for c in range(ROUNDS):
+            chunk = keep.tile([P, ROUND_TILES, NODES], BF16, name="adj_sb%d" % c)
+            nc.sync.dma_start(out=chunk[:], in_=adj_rows[:, c * ROUND_TILES : (c + 1) * ROUND_TILES, :])
+            adj_sb.append(chunk)
+
+        bias_sb = keep.tile([P, HIDDEN], F32)
+        x_grouped, x_codes, x_scales = [], [], []
+        s_grouped, s_codes, s_scales = [], [], []
+        for g in range(NODE_PASSES):
+            x_grouped.append(keep.tile([P, K_PASS, PACK], BF16, name="x_grouped%d" % g, align_bytes=64))
+            x_codes.append(keep.tile([P, K_PASS], U32, name="x_codes%d" % g, align_bytes=64))
+            x_scales.append(keep.tile([P, K_PASS], U8, name="x_scales%d" % g, align_bytes=64))
+            s_grouped.append(keep.tile([P, HIDDEN, PACK], BF16, name="s_grouped%d" % g, align_bytes=64))
+            s_codes.append(keep.tile([P, HIDDEN], U32, name="s_codes%d" % g, align_bytes=64))
+            s_scales.append(keep.tile([P, HIDDEN], U8, name="s_scales%d" % g, align_bytes=64))
+        a_grouped, a_codes, a_scales = {}, {}, {}
+        for c in range(ROUNDS):
+            for g in range(NODE_PASSES):
+                a_grouped[c, g] = keep.tile(
+                    [P, ROUND_TILES * P, PACK], BF16, name="a_grouped%d_%d" % (c, g), align_bytes=64
+                )
+                a_codes[c, g] = keep.tile([P, ROUND_TILES * P], U32, name="a_codes%d_%d" % (c, g), align_bytes=64)
+                a_scales[c, g] = keep.tile([P, ROUND_TILES * P], U8, name="a_scales%d_%d" % (c, g), align_bytes=64)
+
+        def turn_x(g):
+            grouped_words = x_grouped[g][:].bitcast(F32)
+            for u in range(2):
+                words = x_sb[2 * g + u][:].bitcast(F32)
+                bank = banks.tile([P, 2, 2 * P], F32, tag="bank")
+                for e in range(2):
+                    for half in range(2):
+                        nc.tensor.transpose(
+                            bank[:, half, e * P : (e + 1) * P], words[:, e, half : FEATURES // 2 : 2], ident[:]
+                        )
+                empty_bank(u, grouped_words[:, 2 * u * P : 2 * (u + 1) * P, :], bank[:].rearrange("p w c -> p c w"))
+
+        def support_of(g):
+            for hb in range(HIDDEN // P):
+                cols = slice(hb * P, (hb + 1) * P)
+                bank = banks.tile([P, PACK, P], F32, tag="bank")
+                for t in range(PACK):
+                    nodes = slice(t * P, (t + 1) * P)
+                    nc.tensor.matmul_mx(
+                        out=bank[:, t, :],
+                        lhsT=x_codes[g][:, nodes].bitcast(FP8X4),
+                        lhsT_scale=x_scales[g][:, nodes],
+                        rhs=w_codes[:, cols].bitcast(FP8X4),
+                        rhs_scale=w_scales[:, cols],
+                        start=True,
+                        stop=True,
+                    )
+                empty_bank(hb, s_grouped[g][:, cols, :], bank[:].rearrange("p t n -> p n t"))
+
+        def turn_adj(c):
+            words = adj_sb[c][:].bitcast(F32)
+            for g in range(NODE_PASSES):
+                bank = banks.tile([P, 2, ROUND_TILES * P], F32, tag="bank")
+                for s in range(ROUND_TILES):
+                    for u in range(2):
+                        nc.tensor.transpose(
+                            bank[:, u, s * P : (s + 1) * P], words[:, s, 2 * g * P + u : 2 * (g + 1) * P : 2], ident[:]
+                        )
+                nc.scalar.copy(out=a_grouped[c, g][:].bitcast(F32), in_=bank[:].rearrange("p w c -> p c w"))
+
+        def quantise_adj(c):
+            for g in range(NODE_PASSES):
+                quantise(a_grouped[c, g], a_codes[c, g], a_scales[c, g])
+
+        def spread_bias():
+            bank = banks.tile([P, HIDDEN], F32, tag="bank")
+            nc.tensor.matmul(out=bank[:], lhsT=ones[:], rhs=bias_row[:], start=True, stop=True)
+            nc.scalar.copy(out=bias_sb[:], in_=bank[:])
+
+        def output_rows(c):
+            for s in range(ROUND_TILES):
+                r = c * ROUND_TILES + s
+                rows = slice(s * P, (s + 1) * P)
+                result = keep.tile([P, HIDDEN], F32, name="result%d" % r)
+                width = HIDDEN // 2 if r == ROW_TILES - 1 else HIDDEN
+                for first in range(0, HIDDEN, width):
+                    cols = slice(first, first + width)
+                    bank = banks.tile([P, width], F32, tag="bank")
+                    for g in range(NODE_PASSES):
+                        nc.tensor.matmul_mx(
+                            out=bank[:],
+                            lhsT=a_codes[c, g][:, rows].bitcast(FP8X4),
+                            lhsT_scale=a_scales[c, g][:, rows],
+                            rhs=s_codes[g][:, cols].bitcast(FP8X4),
+                            rhs_scale=s_scales[g][:, cols],
+                            start=(g == 0),
+                            stop=(g == NODE_PASSES - 1),
+                        )
+                    nc.vector.tensor_tensor(out=result[:, cols], in0=bank[:], in1=bias_sb[:, cols], op=ALU.add)
+                    if r % 2 == 0:
+                        nc.gpsimd.tensor_scalar(
+                            out=result[:, cols], in0=result[:, cols], scalar1=F32_MAX, scalar2=0.0, op0=ALU.min, op1=ALU.max
+                        )
+                    else:
+                        nc.scalar.activation(out=result[:, cols], in_=result[:, cols], func=ACT.Relu)
+                    nc.sync.dma_start(out=out_rows[:, r, cols], in_=result[:, cols])
+
+        for g in range(NODE_PASSES):
+            if g == NODE_PASSES - 1:
+                spread_bias()
+            turn_x(g)
+            quantise(x_grouped[g], x_codes[g], x_scales[g])
+        for g in range(NODE_PASSES):
+            support_of(g)
+            quantise(s_grouped[g], s_codes[g], s_scales[g])
+        for c in range(AHEAD):
+            turn_adj(c)
+            quantise_adj(c)
+        for c in range(ROUNDS):
+            if c + AHEAD < ROUNDS:
+                turn_adj(c + AHEAD)
+            output_rows(c)
+            if c + AHEAD < ROUNDS:
+                quantise_adj(c + AHEAD)

@@ -22,6 +22,7 @@ NODE_PASSES = NODES // K_PASS
 ROW_TILES = NODES // P
 ROUND_TILES = 2
 ROUNDS = ROW_TILES // ROUND_TILES
+BIAS_BEHIND = 3
 AHEAD = 3
 
 F32_MAX = 3.4028234663852886e38
@@ -49,31 +50,32 @@ def tile_gcn_pa_kernel(tc, x_init, adj1, W1_words, W1_scales, b1, out):
                 in_=grouped[:].rearrange("p c t -> p (c t)"),
             )
 
+        w_scales = keep.tile([P, HIDDEN], U8, align_bytes=64)
+        nc.vector.memset(w_scales[:].bitcast(I32), 0)
         ident = keep.tile([P, P], F32)
         make_identity(nc, ident[:])
-        ones = keep.tile([P, P], BF16)
-        nc.vector.memset(ones[:], 1.0)
-        bias_row = keep.tile([P, HIDDEN], BF16)
-        nc.vector.memset(bias_row[:], 0.0)
-        nc.scalar.dma_start(out=bias_row[0:1, :], in_=b1.rearrange("(o h) -> o h", o=1))
         warm = keep.tile([P, 1], F32)
         nc.vector.memset(warm[:], 0.0)
         nc.scalar.activation(out=warm[:], in_=warm[:], func=ACT.Relu)
 
-        w_scales = keep.tile([P, HIDDEN], U8, align_bytes=64)
-        nc.vector.memset(w_scales[:].bitcast(I32), 0)
 
-        x_chunks = x_init.rearrange("(g p u e) f -> g u p e f", p=P, u=2, e=2)
-        x_sb = []
-        for a in range(2 * NODE_PASSES):
-            chunk = keep.tile([P, 2, FEATURES], BF16, name="x_sb%d" % a)
-            nc.sync.dma_start(out=chunk[:], in_=x_chunks[a // 2, a % 2])
-            x_sb.append(chunk)
+        x_halves = x_init.rearrange("(g p u e) f -> g u p e f", p=P, u=2, e=2)
+        x_whole = x_init.rearrange("(g p e) f -> g p e f", p=P, e=4)
+        x_sb = {}
+        for u in range(2):
+            half = keep.tile([P, 2, FEATURES], BF16, name="x_half%d" % u)
+            nc.sync.dma_start(out=half[:], in_=x_halves[0, u])
+            x_sb[0, u] = half[:]
         for quadrant in range(4):
             nc.sync.dma_start(
                 out=w_scales[32 * quadrant : 32 * quadrant + 4, :].bitcast(I32),
                 in_=W1_scales[0, 4 * quadrant : 4 * quadrant + 4, :].bitcast(I32),
             )
+        for g in range(1, NODE_PASSES):
+            whole = keep.tile([P, 4, FEATURES], BF16, name="x_whole%d" % g)
+            nc.sync.dma_start(out=whole[:], in_=x_whole[g])
+            for u in range(2):
+                x_sb[g, u] = whole[:, 2 * u : 2 * u + 2, :]
         w_codes = keep.tile([P, HIDDEN], U32, align_bytes=64)
         nc.sync.dma_start(out=w_codes[:].bitcast(I32), in_=W1_words[0].rearrange("p n t -> p (n t)").bitcast(I32))
         adj_rows = adj1.rearrange("(p r) k -> p r k", r=ROW_TILES)
@@ -83,8 +85,10 @@ def tile_gcn_pa_kernel(tc, x_init, adj1, W1_words, W1_scales, b1, out):
             chunk = keep.tile([P, ROUND_TILES, NODES], BF16, name="adj_sb%d" % c)
             nc.sync.dma_start(out=chunk[:], in_=adj_rows[:, c * ROUND_TILES : (c + 1) * ROUND_TILES, :])
             adj_sb.append(chunk)
+            if c == BIAS_BEHIND:
+                bias_sb = keep.tile([P, HIDDEN], BF16)
+                nc.sync.dma_start(out=bias_sb[:], in_=b1.partition_broadcast(P))
 
-        bias_sb = keep.tile([P, HIDDEN], F32)
         x_grouped, x_codes, x_scales = [], [], []
         s_grouped, s_codes, s_scales = [], [], []
         for g in range(NODE_PASSES):
@@ -106,7 +110,7 @@ def tile_gcn_pa_kernel(tc, x_init, adj1, W1_words, W1_scales, b1, out):
         def turn_x(g):
             grouped_words = x_grouped[g][:].bitcast(F32)
             for u in range(2):
-                words = x_sb[2 * g + u][:].bitcast(F32)
+                words = x_sb[g, u].bitcast(F32)
                 bank = banks.tile([P, 2, 2 * P], F32, tag="bank")
                 for e in range(2):
                     for half in range(2):
@@ -147,11 +151,6 @@ def tile_gcn_pa_kernel(tc, x_init, adj1, W1_words, W1_scales, b1, out):
             for g in range(NODE_PASSES):
                 quantise(a_grouped[c, g], a_codes[c, g], a_scales[c, g])
 
-        def spread_bias():
-            bank = banks.tile([P, HIDDEN], F32, tag="bank")
-            nc.tensor.matmul(out=bank[:], lhsT=ones[:], rhs=bias_row[:], start=True, stop=True)
-            nc.scalar.copy(out=bias_sb[:], in_=bank[:])
-
         def output_rows(c):
             for s in range(ROUND_TILES):
                 r = c * ROUND_TILES + s
@@ -181,8 +180,6 @@ def tile_gcn_pa_kernel(tc, x_init, adj1, W1_words, W1_scales, b1, out):
                     nc.sync.dma_start(out=out_rows[:, r, cols], in_=result[:, cols])
 
         for g in range(NODE_PASSES):
-            if g == NODE_PASSES - 1:
-                spread_bias()
             turn_x(g)
             quantise(x_grouped[g], x_codes[g], x_scales[g])
         for g in range(NODE_PASSES):

@@ -22,10 +22,9 @@ NODE_PASSES = NODES // K_PASS
 ROW_TILES = NODES // P
 ROUND_TILES = 2
 ROUNDS = ROW_TILES // ROUND_TILES
-BIAS_BEHIND = 3
 AHEAD = 3
-
-F32_MAX = 3.4028234663852886e38
+FIRST_SORTED = 3
+BIAS_BEHIND = 3
 
 FLOPS = 2 * NODES * FEATURES * HIDDEN + 2 * NODES * NODES * HIDDEN
 
@@ -37,11 +36,11 @@ def tile_gcn_pa_kernel(tc, x_init, adj1, W1_words, W1_scales, b1, out):
         banks = ctx.enter_context(tc.psum_pool(name="banks", bufs=8))
         ctx.enter_context(tc.manual_schedule())
 
-        def empty_bank(index, dst, src):
-            if index % 2 == 0:
-                nc.scalar.copy(out=dst, in_=src)
-            else:
-                nc.vector.tensor_copy(out=dst, in_=src)
+        def scalar_copy(dst, src):
+            nc.scalar.copy(out=dst, in_=src)
+
+        def vector_copy(dst, src):
+            nc.vector.tensor_copy(out=dst, in_=src)
 
         def quantise(grouped, codes, scales):
             nc.vector.quantize_mx(
@@ -57,7 +56,6 @@ def tile_gcn_pa_kernel(tc, x_init, adj1, W1_words, W1_scales, b1, out):
         warm = keep.tile([P, 1], F32)
         nc.vector.memset(warm[:], 0.0)
         nc.scalar.activation(out=warm[:], in_=warm[:], func=ACT.Relu)
-
 
         x_halves = x_init.rearrange("(g p u e) f -> g u p e f", p=P, u=2, e=2)
         x_whole = x_init.rearrange("(g p e) f -> g p e f", p=P, e=4)
@@ -78,12 +76,13 @@ def tile_gcn_pa_kernel(tc, x_init, adj1, W1_words, W1_scales, b1, out):
                 x_sb[g, u] = whole[:, 2 * u : 2 * u + 2, :]
         w_codes = keep.tile([P, HIDDEN], U32, align_bytes=64)
         nc.sync.dma_start(out=w_codes[:].bitcast(I32), in_=W1_words[0].rearrange("p n t -> p (n t)").bitcast(I32))
-        adj_rows = adj1.rearrange("(p r) k -> p r k", r=ROW_TILES)
+        adj_rows = adj1.rearrange("(p r) k -> p (r k)", r=ROW_TILES)
         out_rows = out.rearrange("(p r) h -> p r h", r=ROW_TILES)
+        round_width = ROUND_TILES * NODES
         adj_sb = []
         for c in range(ROUNDS):
-            chunk = keep.tile([P, ROUND_TILES, NODES], BF16, name="adj_sb%d" % c)
-            nc.sync.dma_start(out=chunk[:], in_=adj_rows[:, c * ROUND_TILES : (c + 1) * ROUND_TILES, :])
+            chunk = keep.tile([P, round_width], BF16, name="adj_sb%d" % c)
+            nc.sync.dma_start(out=chunk[:], in_=adj_rows[:, c * round_width : (c + 1) * round_width])
             adj_sb.append(chunk)
             if c == BIAS_BEHIND:
                 bias_sb = keep.tile([P, HIDDEN], BF16)
@@ -106,6 +105,7 @@ def tile_gcn_pa_kernel(tc, x_init, adj1, W1_words, W1_scales, b1, out):
                 )
                 a_codes[c, g] = keep.tile([P, ROUND_TILES * P], U32, name="a_codes%d_%d" % (c, g), align_bytes=64)
                 a_scales[c, g] = keep.tile([P, ROUND_TILES * P], U8, name="a_scales%d_%d" % (c, g), align_bytes=64)
+        results = [keep.tile([P, HIDDEN], F32, name="result%d" % r) for r in range(ROW_TILES)]
 
         def turn_x(g):
             grouped_words = x_grouped[g][:].bitcast(F32)
@@ -117,80 +117,122 @@ def tile_gcn_pa_kernel(tc, x_init, adj1, W1_words, W1_scales, b1, out):
                         nc.tensor.transpose(
                             bank[:, half, e * P : (e + 1) * P], words[:, e, half : FEATURES // 2 : 2], ident[:]
                         )
-                empty_bank(u, grouped_words[:, 2 * u * P : 2 * (u + 1) * P, :], bank[:].rearrange("p w c -> p c w"))
+                copy = vector_copy if u == 0 and g < NODE_PASSES - 1 else scalar_copy
+                copy(grouped_words[:, 2 * u * P : 2 * (u + 1) * P, :], bank[:].rearrange("p w c -> p c w"))
 
-        def support_of(g):
-            for hb in range(HIDDEN // P):
-                cols = slice(hb * P, (hb + 1) * P)
-                bank = banks.tile([P, PACK, P], F32, tag="bank")
-                for t in range(PACK):
-                    nodes = slice(t * P, (t + 1) * P)
-                    nc.tensor.matmul_mx(
-                        out=bank[:, t, :],
-                        lhsT=x_codes[g][:, nodes].bitcast(FP8X4),
-                        lhsT_scale=x_scales[g][:, nodes],
-                        rhs=w_codes[:, cols].bitcast(FP8X4),
-                        rhs_scale=w_scales[:, cols],
-                        start=True,
-                        stop=True,
-                    )
-                empty_bank(hb, s_grouped[g][:, cols, :], bank[:].rearrange("p t n -> p n t"))
+        def quantise_x(g):
+            quantise(x_grouped[g], x_codes[g], x_scales[g])
+
+        def support_columns(g, hb):
+            cols = slice(hb * P, (hb + 1) * P)
+            bank = banks.tile([P, PACK, P], F32, tag="bank")
+            for t in range(PACK):
+                nodes = slice(t * P, (t + 1) * P)
+                nc.tensor.matmul_mx(
+                    out=bank[:, t, :],
+                    lhsT=x_codes[g][:, nodes].bitcast(FP8X4),
+                    lhsT_scale=x_scales[g][:, nodes],
+                    rhs=w_codes[:, cols].bitcast(FP8X4),
+                    rhs_scale=w_scales[:, cols],
+                    start=True,
+                    stop=True,
+                )
+            copy = vector_copy if hb % 2 == 1 else scalar_copy
+            copy(s_grouped[g][:, cols, :], bank[:].rearrange("p t n -> p n t"))
+
+        def quantise_support(g):
+            quantise(s_grouped[g], s_codes[g], s_scales[g])
+
+        def sort_adj(c):
+            if FIRST_SORTED <= c < ROUNDS:
+                blocks = ROUND_TILES * NODE_PASSES
+                chunk = keep.tile([P, blocks, 2, P], F32, name="adj_sorted%d" % c)
+                nc.vector.tensor_copy(
+                    out=chunk[:], in_=adj_sb[c][:].bitcast(F32).rearrange("p (b w u) -> p b u w", b=blocks, u=2)
+                )
+                adj_sorted[c] = chunk
 
         def turn_adj(c):
             words = adj_sb[c][:].bitcast(F32)
             for g in range(NODE_PASSES):
                 bank = banks.tile([P, 2, ROUND_TILES * P], F32, tag="bank")
                 for s in range(ROUND_TILES):
+                    block = s * NODE_PASSES + g
                     for u in range(2):
-                        nc.tensor.transpose(
-                            bank[:, u, s * P : (s + 1) * P], words[:, s, 2 * g * P + u : 2 * (g + 1) * P : 2], ident[:]
-                        )
-                nc.scalar.copy(out=a_grouped[c, g][:].bitcast(F32), in_=bank[:].rearrange("p w c -> p c w"))
+                        if c in adj_sorted:
+                            source = adj_sorted[c][:, block, u, :]
+                        else:
+                            source = words[:, 2 * block * P + u : 2 * (block + 1) * P : 2]
+                        nc.tensor.transpose(bank[:, u, s * P : (s + 1) * P], source, ident[:])
+                scalar_copy(a_grouped[c, g][:].bitcast(F32), bank[:].rearrange("p w c -> p c w"))
 
         def quantise_adj(c):
             for g in range(NODE_PASSES):
                 quantise(a_grouped[c, g], a_codes[c, g], a_scales[c, g])
 
-        def output_rows(c):
-            for s in range(ROUND_TILES):
-                r = c * ROUND_TILES + s
-                rows = slice(s * P, (s + 1) * P)
-                result = keep.tile([P, HIDDEN], F32, name="result%d" % r)
-                width = HIDDEN // 2 if r == ROW_TILES - 1 else HIDDEN
-                for first in range(0, HIDDEN, width):
-                    cols = slice(first, first + width)
-                    bank = banks.tile([P, width], F32, tag="bank")
-                    for g in range(NODE_PASSES):
-                        nc.tensor.matmul_mx(
-                            out=bank[:],
-                            lhsT=a_codes[c, g][:, rows].bitcast(FP8X4),
-                            lhsT_scale=a_scales[c, g][:, rows],
-                            rhs=s_codes[g][:, cols].bitcast(FP8X4),
-                            rhs_scale=s_scales[g][:, cols],
-                            start=(g == 0),
-                            stop=(g == NODE_PASSES - 1),
-                        )
-                    nc.vector.tensor_tensor(out=result[:, cols], in0=bank[:], in1=bias_sb[:, cols], op=ALU.add)
-                    if r % 2 == 0:
-                        nc.gpsimd.tensor_scalar(
-                            out=result[:, cols], in0=result[:, cols], scalar1=F32_MAX, scalar2=0.0, op0=ALU.min, op1=ALU.max
-                        )
-                    else:
-                        nc.scalar.activation(out=result[:, cols], in_=result[:, cols], func=ACT.Relu)
-                    nc.sync.dma_start(out=out_rows[:, r, cols], in_=result[:, cols])
+        def multiply(r, cols):
+            c, s = divmod(r, ROUND_TILES)
+            rows = slice(s * P, (s + 1) * P)
+            bank = banks.tile([P, cols.stop - cols.start], F32, tag="bank")
+            for g in range(NODE_PASSES):
+                nc.tensor.matmul_mx(
+                    out=bank[:],
+                    lhsT=a_codes[c, g][:, rows].bitcast(FP8X4),
+                    lhsT_scale=a_scales[c, g][:, rows],
+                    rhs=s_codes[g][:, cols].bitcast(FP8X4),
+                    rhs_scale=s_scales[g][:, cols],
+                    start=(g == 0),
+                    stop=(g == NODE_PASSES - 1),
+                )
+            return bank
 
+        def add_bias(r, cols, bank):
+            nc.vector.tensor_tensor(out=results[r][:, cols], in0=bank[:], in1=bias_sb[:, cols], op=ALU.add)
+
+        def store(r, cols):
+            nc.scalar.activation(out=results[r][:, cols], in_=results[r][:, cols], func=ACT.Relu)
+            nc.sync.dma_start(out=out_rows[:, r, cols], in_=results[r][:, cols])
+
+        adj_sorted = {}
+        everything = slice(0, HIDDEN)
+        turn_x(0)
+        turn_x(1)
+        quantise_x(0)
+        turn_x(2)
+        quantise_x(1)
         for g in range(NODE_PASSES):
-            turn_x(g)
-            quantise(x_grouped[g], x_codes[g], x_scales[g])
-        for g in range(NODE_PASSES):
-            support_of(g)
-            quantise(s_grouped[g], s_codes[g], s_scales[g])
-        for c in range(AHEAD):
+            for hb in range(HIDDEN // P):
+                support_columns(g, hb)
+                if hb == 1:
+                    if g == 0:
+                        quantise_x(NODE_PASSES - 1)
+                    else:
+                        quantise_support(g - 1)
+        turn_adj(0)
+        quantise_support(NODE_PASSES - 1)
+        for c in range(1, AHEAD):
             turn_adj(c)
-            quantise_adj(c)
+            quantise_adj(c - 1)
+        sort_adj(AHEAD)
         for c in range(ROUNDS):
+            first, second = ROUND_TILES * c, ROUND_TILES * c + 1
             if c + AHEAD < ROUNDS:
+                first_bank = multiply(first, everything)
+                second_bank = multiply(second, everything)
+                add_bias(first, everything, first_bank)
+                quantise_adj(c + AHEAD - 1)
+                add_bias(second, everything, second_bank)
                 turn_adj(c + AHEAD)
-            output_rows(c)
-            if c + AHEAD < ROUNDS:
-                quantise_adj(c + AHEAD)
+                store(first, everything)
+                store(second, everything)
+                sort_adj(c + AHEAD + 1)
+            else:
+                add_bias(first, everything, multiply(first, everything))
+                store(first, everything)
+                if c + AHEAD == ROUNDS:
+                    quantise_adj(ROUNDS - 1)
+                width = HIDDEN // 2 if second == ROW_TILES - 1 else HIDDEN
+                for start in range(0, HIDDEN, width):
+                    cols = slice(start, start + width)
+                    add_bias(second, cols, multiply(second, cols))
+                    store(second, cols)

@@ -58,24 +58,19 @@ def tile_gcn_pa_kernel(tc, x_init, adj1, W1_words, W1_scales, b1, out):
         nc.scalar.activation(out=warm[:], in_=warm[:], func=ACT.Relu)
 
         x_halves = x_init.rearrange("(g p u e) f -> g u p e f", p=P, u=2, e=2)
-        x_whole = x_init.rearrange("(g p e) f -> g p e f", p=P, e=4)
         x_sb = {}
-        for u in range(2):
-            half = keep.tile([P, 2, FEATURES], BF16, name="x_half%d" % u)
-            nc.sync.dma_start(out=half[:], in_=x_halves[0, u])
-            x_sb[0, u] = half[:]
+        for g in range(NODE_PASSES):
+            for u in range(2):
+                half = keep.tile([P, 2, FEATURES], BF16, name="x_sb%d_%d" % (g, u))
+                nc.sync.dma_start(out=half[:], in_=x_halves[g, u])
+                x_sb[g, u] = half
+        w_codes = keep.tile([P, HIDDEN], U32, align_bytes=64)
+        nc.sync.dma_start(out=w_codes[:].bitcast(I32), in_=W1_words[0].rearrange("p n t -> p (n t)").bitcast(I32))
         for quadrant in range(4):
             nc.sync.dma_start(
                 out=w_scales[32 * quadrant : 32 * quadrant + 4, :].bitcast(I32),
                 in_=W1_scales[0, 4 * quadrant : 4 * quadrant + 4, :].bitcast(I32),
             )
-        for g in range(1, NODE_PASSES):
-            whole = keep.tile([P, 4, FEATURES], BF16, name="x_whole%d" % g)
-            nc.sync.dma_start(out=whole[:], in_=x_whole[g])
-            for u in range(2):
-                x_sb[g, u] = whole[:, 2 * u : 2 * u + 2, :]
-        w_codes = keep.tile([P, HIDDEN], U32, align_bytes=64)
-        nc.sync.dma_start(out=w_codes[:].bitcast(I32), in_=W1_words[0].rearrange("p n t -> p (n t)").bitcast(I32))
         adj_rows = adj1.rearrange("(p r) k -> p (r k)", r=ROW_TILES)
         out_rows = out.rearrange("(p r) h -> p r h", r=ROW_TILES)
         round_width = ROUND_TILES * NODES
@@ -110,7 +105,7 @@ def tile_gcn_pa_kernel(tc, x_init, adj1, W1_words, W1_scales, b1, out):
         def turn_x(g):
             grouped_words = x_grouped[g][:].bitcast(F32)
             for u in range(2):
-                words = x_sb[g, u].bitcast(F32)
+                words = x_sb[g, u][:].bitcast(F32)
                 bank = banks.tile([P, 2, 2 * P], F32, tag="bank")
                 for e in range(2):
                     for half in range(2):
@@ -148,7 +143,8 @@ def tile_gcn_pa_kernel(tc, x_init, adj1, W1_words, W1_scales, b1, out):
                 blocks = ROUND_TILES * NODE_PASSES
                 chunk = keep.tile([P, blocks, 2, P], F32, name="adj_sorted%d" % c)
                 nc.vector.tensor_copy(
-                    out=chunk[:], in_=adj_sb[c][:].bitcast(F32).rearrange("p (b w u) -> p b u w", b=blocks, u=2)
+                    out=chunk[:].rearrange("p b u w -> p b w u"),
+                    in_=adj_sb[c][:].bitcast(F32).rearrange("p (b w u) -> p b w u", b=blocks, u=2),
                 )
                 adj_sorted[c] = chunk
 

from contextlib import ExitStack

import concourse.mybir as mybir
from concourse.masks import make_identity

F32 = mybir.dt.float32
BF16 = mybir.dt.bfloat16
I32 = mybir.dt.int32
U32 = mybir.dt.uint32
U8 = mybir.dt.uint8
FP8X4 = mybir.dt.float8_e4m3fn_x4
ALU = mybir.AluOpType
ACT = mybir.ActivationFunctionType

P = 128
PACK = 4
K_PASS = P * PACK
NODES = 1536
FEATURES = 512
HIDDEN = 512
NODE_PASSES = NODES // K_PASS
ROW_TILES = NODES // P
ROUND_TILES = 2
ROUNDS = ROW_TILES // ROUND_TILES
AHEAD = 3
FIRST_SORTED = 3
BIAS_BEHIND = 3

FLOPS = 2 * NODES * FEATURES * HIDDEN + 2 * NODES * NODES * HIDDEN


def tile_gcn_pa_kernel(tc, x_init, adj1, W1_words, W1_scales, b1, out):
    nc = tc.nc
    with ExitStack() as ctx:
        keep = ctx.enter_context(tc.tile_pool(name="keep", bufs=1))
        banks = ctx.enter_context(tc.psum_pool(name="banks", bufs=8))
        ctx.enter_context(tc.manual_schedule())

        def scalar_copy(dst, src):
            nc.scalar.copy(out=dst, in_=src)

        def vector_copy(dst, src):
            nc.vector.tensor_copy(out=dst, in_=src)

        def quantise(grouped, codes, scales):
            nc.vector.quantize_mx(
                out=codes[:].bitcast(FP8X4),
                scales=scales[:],
                in_=grouped[:].rearrange("p c t -> p (c t)"),
            )

        w_scales = keep.tile([P, HIDDEN], U8, align_bytes=64)
        nc.vector.memset(w_scales[:].bitcast(I32), 0)
        ident = keep.tile([P, P], F32)
        make_identity(nc, ident[:])
        warm = keep.tile([P, 1], F32)
        nc.vector.memset(warm[:], 0.0)
        nc.scalar.activation(out=warm[:], in_=warm[:], func=ACT.Relu)

        x_halves = x_init.rearrange("(g p u e) f -> g u p e f", p=P, u=2, e=2)
        x_sb = {}
        for g in range(NODE_PASSES):
            for u in range(2):
                half = keep.tile([P, 2, FEATURES], BF16, name="x_sb%d_%d" % (g, u))
                nc.sync.dma_start(out=half[:], in_=x_halves[g, u])
                x_sb[g, u] = half
        w_codes = keep.tile([P, HIDDEN], U32, align_bytes=64)
        nc.sync.dma_start(out=w_codes[:].bitcast(I32), in_=W1_words[0].rearrange("p n t -> p (n t)").bitcast(I32))
        for quadrant in range(4):
            nc.sync.dma_start(
                out=w_scales[32 * quadrant : 32 * quadrant + 4, :].bitcast(I32),
                in_=W1_scales[0, 4 * quadrant : 4 * quadrant + 4, :].bitcast(I32),
            )
        adj_rows = adj1.rearrange("(p r) k -> p (r k)", r=ROW_TILES)
        out_rows = out.rearrange("(p r) h -> p r h", r=ROW_TILES)
        round_width = ROUND_TILES * NODES
        adj_sb = []
        for c in range(ROUNDS):
            chunk = keep.tile([P, round_width], BF16, name="adj_sb%d" % c)
            nc.sync.dma_start(out=chunk[:], in_=adj_rows[:, c * round_width : (c + 1) * round_width])
            adj_sb.append(chunk)
            if c == BIAS_BEHIND:
                bias_sb = keep.tile([P, HIDDEN], BF16)
                nc.sync.dma_start(out=bias_sb[:], in_=b1.partition_broadcast(P))

        x_grouped, x_codes, x_scales = [], [], []
        s_grouped, s_codes, s_scales = [], [], []
        for g in range(NODE_PASSES):
            x_grouped.append(keep.tile([P, K_PASS, PACK], BF16, name="x_grouped%d" % g, align_bytes=64))
            x_codes.append(keep.tile([P, K_PASS], U32, name="x_codes%d" % g, align_bytes=64))
            x_scales.append(keep.tile([P, K_PASS], U8, name="x_scales%d" % g, align_bytes=64))
            s_grouped.append(keep.tile([P, HIDDEN, PACK], BF16, name="s_grouped%d" % g, align_bytes=64))
            s_codes.append(keep.tile([P, HIDDEN], U32, name="s_codes%d" % g, align_bytes=64))
            s_scales.append(keep.tile([P, HIDDEN], U8, name="s_scales%d" % g, align_bytes=64))
        a_grouped, a_codes, a_scales = {}, {}, {}
        for c in range(ROUNDS):
            for g in range(NODE_PASSES):
                a_grouped[c, g] = keep.tile(
                    [P, ROUND_TILES * P, PACK], BF16, name="a_grouped%d_%d" % (c, g), align_bytes=64
                )
                a_codes[c, g] = keep.tile([P, ROUND_TILES * P], U32, name="a_codes%d_%d" % (c, g), align_bytes=64)
                a_scales[c, g] = keep.tile([P, ROUND_TILES * P], U8, name="a_scales%d_%d" % (c, g), align_bytes=64)
        results = [keep.tile([P, HIDDEN], F32, name="result%d" % r) for r in range(ROW_TILES)]

        def turn_x(g):
            grouped_words = x_grouped[g][:].bitcast(F32)
            for u in range(2):
                words = x_sb[g, u][:].bitcast(F32)
                bank = banks.tile([P, 2, 2 * P], F32, tag="bank")
                for e in range(2):
                    for half in range(2):
                        nc.tensor.transpose(
                            bank[:, half, e * P : (e + 1) * P], words[:, e, half : FEATURES // 2 : 2], ident[:]
                        )
                copy = vector_copy if u == 0 and g < NODE_PASSES - 1 else scalar_copy
                copy(grouped_words[:, 2 * u * P : 2 * (u + 1) * P, :], bank[:].rearrange("p w c -> p c w"))

        def quantise_x(g):
            quantise(x_grouped[g], x_codes[g], x_scales[g])

        def support_columns(g, hb):
            cols = slice(hb * P, (hb + 1) * P)
            bank = banks.tile([P, PACK, P], F32, tag="bank")
            for t in range(PACK):
                nodes = slice(t * P, (t + 1) * P)
                nc.tensor.matmul_mx(
                    out=bank[:, t, :],
                    lhsT=x_codes[g][:, nodes].bitcast(FP8X4),
                    lhsT_scale=x_scales[g][:, nodes],
                    rhs=w_codes[:, cols].bitcast(FP8X4),
                    rhs_scale=w_scales[:, cols],
                    start=True,
                    stop=True,
                )
            copy = vector_copy if hb % 2 == 1 else scalar_copy
            copy(s_grouped[g][:, cols, :], bank[:].rearrange("p t n -> p n t"))

        def quantise_support(g):
            quantise(s_grouped[g], s_codes[g], s_scales[g])

        def sort_adj(c):
            if FIRST_SORTED <= c < ROUNDS:
                blocks = ROUND_TILES * NODE_PASSES
                chunk = keep.tile([P, blocks, 2, P], F32, name="adj_sorted%d" % c)
                nc.vector.tensor_copy(
                    out=chunk[:].rearrange("p b u w -> p b w u"),
                    in_=adj_sb[c][:].bitcast(F32).rearrange("p (b w u) -> p b w u", b=blocks, u=2),
                )
                adj_sorted[c] = chunk

        def turn_adj(c):
            words = adj_sb[c][:].bitcast(F32)
            for g in range(NODE_PASSES):
                bank = banks.tile([P, 2, ROUND_TILES * P], F32, tag="bank")
                for s in range(ROUND_TILES):
                    block = s * NODE_PASSES + g
                    for u in range(2):
                        if c in adj_sorted:
                            source = adj_sorted[c][:, block, u, :]
                        else:
                            source = words[:, 2 * block * P + u : 2 * (block + 1) * P : 2]
                        nc.tensor.transpose(bank[:, u, s * P : (s + 1) * P], source, ident[:])
                scalar_copy(a_grouped[c, g][:].bitcast(F32), bank[:].rearrange("p w c -> p c w"))

        def quantise_adj(c):
            for g in range(NODE_PASSES):
                quantise(a_grouped[c, g], a_codes[c, g], a_scales[c, g])

        def multiply(r, cols):
            c, s = divmod(r, ROUND_TILES)
            rows = slice(s * P, (s + 1) * P)
            bank = banks.tile([P, cols.stop - cols.start], F32, tag="bank")
            for g in range(NODE_PASSES):
                nc.tensor.matmul_mx(
                    out=bank[:],
                    lhsT=a_codes[c, g][:, rows].bitcast(FP8X4),
                    lhsT_scale=a_scales[c, g][:, rows],
                    rhs=s_codes[g][:, cols].bitcast(FP8X4),
                    rhs_scale=s_scales[g][:, cols],
                    start=(g == 0),
                    stop=(g == NODE_PASSES - 1),
                )
            return bank

        def add_bias(r, cols, bank):
            nc.vector.tensor_tensor(out=results[r][:, cols], in0=bank[:], in1=bias_sb[:, cols], op=ALU.add)

        def store(r, cols):
            nc.scalar.activation(out=results[r][:, cols], in_=results[r][:, cols], func=ACT.Relu)
            nc.sync.dma_start(out=out_rows[:, r, cols], in_=results[r][:, cols])

        adj_sorted = {}
        everything = slice(0, HIDDEN)
        turn_x(0)
        turn_x(1)
        quantise_x(0)
        turn_x(2)
        quantise_x(1)
        for g in range(NODE_PASSES):
            for hb in range(HIDDEN // P):
                support_columns(g, hb)
                if hb == 1:
                    if g == 0:
                        quantise_x(NODE_PASSES - 1)
                    else:
                        quantise_support(g - 1)
        turn_adj(0)
        quantise_support(NODE_PASSES - 1)
        for c in range(1, AHEAD):
            turn_adj(c)
            quantise_adj(c - 1)
        sort_adj(AHEAD)
        for c in range(ROUNDS):
            first, second = ROUND_TILES * c, ROUND_TILES * c + 1
            if c + AHEAD < ROUNDS:
                first_bank = multiply(first, everything)
                second_bank = multiply(second, everything)
                add_bias(first, everything, first_bank)
                quantise_adj(c + AHEAD - 1)
                add_bias(second, everything, second_bank)
                turn_adj(c + AHEAD)
                store(first, everything)
                store(second, everything)
                sort_adj(c + AHEAD + 1)
            else:
                add_bias(first, everything, multiply(first, everything))
                store(first, everything)
                if c + AHEAD == ROUNDS:
                    quantise_adj(ROUNDS - 1)
                width = HIDDEN // 2 if second == ROW_TILES - 1 else HIDDEN
                for start in range(0, HIDDEN, width):
                    cols = slice(start, start + width)
                    add_bias(second, cols, multiply(second, cols))
                    store(second, cols)
